import numpy as np
import ml_dtypes


def mxq(x, axis, fmt="e4m3"):
    dtype, down = {"e4m3": (ml_dtypes.float8_e4m3fn, 7), "e5m2": (ml_dtypes.float8_e5m2, 14)}[fmt]
    v = np.moveaxis(np.asarray(x, np.float32).astype(ml_dtypes.bfloat16).astype(np.float64), axis, -1)
    blocks = v.reshape(v.shape[:-1] + (-1, 32))
    amax = np.abs(blocks).max(-1, keepdims=True)
    byte = np.maximum(np.where(amax > 0, np.frexp(amax)[1] - 1 + 127, 0) - down, 1)
    scale = np.exp2(byte - 127.0)
    codes = (blocks / scale).astype(np.float32).astype(dtype).astype(np.float64)
    return np.moveaxis((codes * scale).reshape(v.shape), -1, axis)


WIDE = False


def mx_kscale(k):
    if not WIDE:
        return np.ones(k)
    levels = np.array([20, -20, 10, -10, 0])
    a = np.random.permutation(np.resize(levels, k // 512 * 4)).reshape(k // 512, 4)
    idx = np.arange(k)
    return np.exp2(a[idx // 512, idx % 128 // 32])


BF16 = ml_dtypes.bfloat16


def bf(x):
    return np.asarray(x, np.float32).astype(BF16)


def f64(x):
    return np.asarray(x).astype(np.float64)


B, CIN, COUT, T, F, KH, KW, PH, PW = 2, 128, 512, 64, 4, 3, 3, 1, 1
OT = T + PH + PH - KH + 1


def setup_inputs():
    u = mx_kscale(COUT)
    x = np.random.standard_normal((B, CIN, T, F))
    kernel = np.random.standard_normal((COUT, CIN, F, KH, KW)) / np.sqrt(CIN * KH * KW) / u[:, None, None, None, None]
    bias = np.random.standard_normal((1, COUT, 1, F)) * 0.5
    g = np.random.standard_normal((B, COUT, OT, F)) * np.exp2(np.random.randint(-12, 1, (B, 1, OT, F))) * 16.0 * u[None, :, None, None]
    return {"x": bf(x), "kernel": bf(kernel), "bias": bf(bias), "grad_out": bf(g)}


def reference(x, kernel, bias, grad_out):
    gq = mxq(f64(grad_out).transpose(3, 2, 0, 1).reshape(F, OT * B, COUT), 2, "e5m2")
    kt = f64(kernel).transpose(2, 3, 4, 0, 1)
    gx = np.zeros((F, T * B, CIN))
    for m in range(KH):
        for n in range(KW):
            f0, f1 = max(0, PW - n), min(F, F + PW - n)
            t0, t1 = max(0, PH - m), min(OT, T + PH - m)
            p = gq[f0:f1] @ mxq(kt[f0:f1, m, n], 1, "e4m3")
            gx[f0 + n - PW:f1 + n - PW, (t0 + m - PH) * B:(t1 + m - PH) * B] += p[:, t0 * B:t1 * B]
    return np.ascontiguousarray(gx.reshape(F, T, B, CIN).transpose(2, 3, 1, 0))

@@ -1,0 +1,162 @@
+import concourse.mybir as mybir
+from concourse.masks import make_identity
+
+BF16 = mybir.dt.bfloat16
+F32 = mybir.dt.float32
+I32 = mybir.dt.int32
+U32 = mybir.dt.uint32
+U8 = mybir.dt.uint8
+E4M3_X4 = mybir.dt.float8_e4m3fn_x4
+E5M2_X4 = mybir.dt.float8_e5m2_x4
+
+P = 128
+PACK = 4
+B, CIN, COUT, T, F, KH, KW = 2, 128, 512, 64, 4, 3, 3
+COLS = B * T
+
+HALF = 64
+HALVES = CIN // HALF
+I_CHUNK = 16
+CHUNKS = CIN // I_CHUNK
+CHUNKS_PER_HALF = HALF // I_CHUNK
+
+VECTOR_BINS = (0, 3)
+SCALAR_BINS = (1, 2)
+
+FLOPS = 2 * 30 * COUT * CIN * COLS
+BYTES = 2 * B * COUT * T * F + 2 * 30 * COUT * CIN + 4 * B * CIN * T * F
+
+
+def first_tap(g):
+    return max(0, 1 - g)
+
+
+def tap_count(g):
+    return min(KW, F + 1 - g) - first_tap(g)
+
+
+def first_out_bin(g):
+    return g + first_tap(g) - 1
+
+
+def tile_svconv2d_pa_s_kernel(tc, x, kernel, bias, grad_out, out):
+    nc = tc.nc
+    with tc.tile_pool(name="keep", bufs=1) as keep, tc.psum_pool(name="psum", bufs=1) as psum:
+        g_raw = keep.tile([P, B, PACK, T, F], BF16)
+        g_grouped = keep.tile([P, KH, F, B, T, PACK], BF16, align_bytes=64)
+        g_codes = keep.tile([P, KH, F, COLS], U32, align_bytes=64)
+        g_scales = keep.tile([P, KH, F, COLS], U8, align_bytes=64)
+
+        w_raw = [
+            keep.tile([P, PACK, I_CHUNK, F, KH, KW], BF16, name="w_raw%d" % c)
+            for c in range(CHUNKS)
+        ]
+        w_grouped = {
+            (g, h): keep.tile(
+                [P, KH, tap_count(g), HALF, PACK], BF16, name="w_grouped%d%d" % (g, h), align_bytes=64
+            )
+            for g in range(F)
+            for h in range(HALVES)
+        }
+        w_codes = keep.tile([P, F, KH, HALVES, F, HALF], U32, align_bytes=64)
+        w_scales = keep.tile([P, F, KH, HALVES, F, HALF], U8, align_bytes=64)
+
+        identity = keep.tile([P, P], F32)
+        sums = keep.tile([P, F, CIN], F32)
+        result = keep.tile([P, B * T, F], F32)
+        acc = psum.tile([P, HALVES, F, HALF], F32)
+        flipped = psum.tile([P, F, COLS], F32)
+
+        for b in range(B):
+            nc.sync.dma_start(
+                out=g_raw[:, b].rearrange("p j t g -> p (j t g)"),
+                in_=grad_out[b].rearrange("(p j) t g -> p (j t g)", j=PACK),
+            )
+        kernel_rows = kernel.rearrange("(p j) i g m n -> p j i (g m n)", j=PACK)
+        for c in range(CHUNKS):
+            nc.sync.dma_start(
+                out=w_raw[c].rearrange("p j i g m n -> p j (i g m n)"),
+                in_=kernel_rows[:, :, c * I_CHUNK : (c + 1) * I_CHUNK, :].rearrange("p j i s -> p j (i s)"),
+            )
+
+        nc.vector.memset(g_grouped[:, 0, :, :, T - 1, :], 0.0)
+        nc.vector.memset(g_grouped[:, 2, :, :, 0, :], 0.0)
+        for g in range(F):
+            lo, hi = first_out_bin(g), first_out_bin(g) + tap_count(g)
+            for f0, f1 in ((0, lo), (hi, F)):
+                if f0 < f1:
+                    nc.vector.memset(
+                        w_codes[:, g, :, :, f0:f1, :].rearrange("p m h f i -> p (m h) (f i)").bitcast(I32), 0
+                    )
+                    nc.vector.memset(
+                        w_scales[:, g, :, :, f0:f1, :].rearrange("p m h f i -> p (m h) (f i)").bitcast(I32), 0
+                    )
+        make_identity(nc, identity[:])
+
+        for b in range(B):
+            nc.vector.tensor_copy(
+                out=g_grouped[:, 1, :, b].rearrange("p g t j -> p t j g"),
+                in_=g_raw[:, b].rearrange("p j t g -> p t j g"),
+            )
+        nc.vector.tensor_copy(out=g_grouped[:, 0, :, :, 0 : T - 1, :], in_=g_grouped[:, 1, :, :, 1:T, :])
+        nc.vector.tensor_copy(out=g_grouped[:, 2, :, :, 1:T, :], in_=g_grouped[:, 1, :, :, 0 : T - 1, :])
+        for m in (1, 0, 2):
+            nc.vector.quantize_mx(
+                out=g_codes[:, m].rearrange("p g c -> p (g c)").bitcast(E5M2_X4),
+                scales=g_scales[:, m].rearrange("p g c -> p (g c)"),
+                in_=g_grouped[:, m].rearrange("p g b t j -> p (g b t j)"),
+            )
+
+        def quantise_half(g, m, h):
+            for n0 in range(0, tap_count(g), 2):
+                n1 = min(n0 + 2, tap_count(g))
+                f0, f1 = first_out_bin(g) + n0, first_out_bin(g) + n1
+                nc.vector.quantize_mx(
+                    out=w_codes[:, g, m, h, f0:f1, :].rearrange("p f i -> p (f i)").bitcast(E4M3_X4),
+                    scales=w_scales[:, g, m, h, f0:f1, :].rearrange("p f i -> p (f i)"),
+                    in_=w_grouped[(g, h)][:, m, n0:n1].rearrange("p n i j -> p (n i j)"),
+                )
+
+        for c in range(CHUNKS):
+            h = c // CHUNKS_PER_HALF
+            i0 = (c % CHUNKS_PER_HALF) * I_CHUNK
+            for g in VECTOR_BINS:
+                n0, n1 = first_tap(g), first_tap(g) + tap_count(g)
+                nc.vector.tensor_copy(
+                    out=w_grouped[(g, h)][:, :, :, i0 : i0 + I_CHUNK, :].rearrange("p m n i j -> p m i j n"),
+                    in_=w_raw[c][:, :, :, g, :, n0:n1].rearrange("p j i m n -> p m i j n"),
+                )
+            for g in SCALAR_BINS:
+                n0, n1 = first_tap(g), first_tap(g) + tap_count(g)
+                for m in range(KH):
+                    nc.scalar.copy(
+                        out=w_grouped[(g, h)][:, m, :, i0 : i0 + I_CHUNK, :].rearrange("p n i j -> p i j n"),
+                        in_=w_raw[c][:, :, :, g, m, n0:n1].rearrange("p j i n -> p i j n"),
+                    )
+            if (c + 1) % CHUNKS_PER_HALF == 0:
+                for g in VECTOR_BINS + SCALAR_BINS:
+                    for m in range(KH):
+                        quantise_half(g, m, h)
+
+        pairs = [(g, m) for g in VECTOR_BINS + SCALAR_BINS for m in range(KH)]
+        for g, m in pairs:
+            nc.tensor.matmul_mx(
+                out=acc[:].rearrange("p h f i -> p (h f i)"),
+                lhsT=g_codes[:, m, g, :].bitcast(E5M2_X4),
+                lhsT_scale=g_scales[:, m, g, :],
+                rhs=w_codes[:, g, m].rearrange("p h f i -> p (h f i)").bitcast(E4M3_X4),
+                rhs_scale=w_scales[:, g, m].rearrange("p h f i -> p (h f i)"),
+                start=((g, m) == pairs[0]),
+                stop=((g, m) == pairs[-1]),
+            )
+
+        for f in range(F):
+            nc.vector.tensor_copy(
+                out=sums[:, f, :].rearrange("p (h i) -> p h i", h=HALVES), in_=acc[:, :, f, :]
+            )
+            nc.tensor.transpose(flipped[:, f, :], sums[:, f, :], identity[:])
+        nc.vector.tensor_copy(out=result[:], in_=flipped[:].rearrange("p f c -> p c f"))
+        nc.sync.dma_start(
+            out=out.rearrange("b i t f -> i b (t f)"),
+            in_=result[:].rearrange("p (b t) f -> p b (t f)", b=B),
+        )

@@ -8,17 +8,19 @@ U32 = mybir.dt.uint32
 U8 = mybir.dt.uint8
 E4M3_X4 = mybir.dt.float8_e4m3fn_x4
 E5M2_X4 = mybir.dt.float8_e5m2_x4
+ADD = mybir.AluOpType.add
 
 P = 128
 PACK = 4
 B, CIN, COUT, T, F, KH, KW = 2, 128, 512, 64, 4, 3, 3
 COLS = B * T
 
-HALF = 64
-HALVES = CIN // HALF
 I_CHUNK = 16
 CHUNKS = CIN // I_CHUNK
-CHUNKS_PER_HALF = HALF // I_CHUNK
+M_SLOTS = 4
+PAIR = 2
+PAIRS = CHUNKS // PAIR
+GROUPED_BUFS = 4
 
 VECTOR_BINS = (0, 3)
 SCALAR_BINS = (1, 2)
@@ -39,124 +41,165 @@ def first_out_bin(g):
     return g + first_tap(g) - 1
 
 
+def first_block(g):
+    return sum(tap_count(k) for k in range(g))
+
+
 def tile_svconv2d_pa_s_kernel(tc, x, kernel, bias, grad_out, out):
     nc = tc.nc
     with tc.tile_pool(name="keep", bufs=1) as keep, tc.psum_pool(name="psum", bufs=1) as psum:
         g_raw = keep.tile([P, B, PACK, T, F], BF16)
-        g_grouped = keep.tile([P, KH, F, B, T, PACK], BF16, align_bytes=64)
-        g_codes = keep.tile([P, KH, F, COLS], U32, align_bytes=64)
-        g_scales = keep.tile([P, KH, F, COLS], U8, align_bytes=64)
+        g_grouped = keep.tile([P, F, B, T, PACK], BF16, align_bytes=64)
+        g_codes = keep.tile([P, F, COLS], U32, align_bytes=64)
+        g_scales = keep.tile([P, F, COLS], U8, align_bytes=64)
 
         w_raw = [
             keep.tile([P, PACK, I_CHUNK, F, KH, KW], BF16, name="w_raw%d" % c)
             for c in range(CHUNKS)
         ]
-        w_grouped = {
-            (g, h): keep.tile(
-                [P, KH, tap_count(g), HALF, PACK], BF16, name="w_grouped%d%d" % (g, h), align_bytes=64
-            )
-            for g in range(F)
-            for h in range(HALVES)
-        }
-        w_codes = keep.tile([P, F, KH, HALVES, F, HALF], U32, align_bytes=64)
-        w_scales = keep.tile([P, F, KH, HALVES, F, HALF], U8, align_bytes=64)
+        w_grouped = [
+            keep.tile([P, first_block(F), M_SLOTS, I_CHUNK, PACK], BF16, name="w_grouped%d" % k, align_bytes=64)
+            for k in range(GROUPED_BUFS)
+        ]
+        w_codes = keep.tile([P, PAIRS, F, PAIR, F, M_SLOTS, I_CHUNK], U32, align_bytes=64)
+        w_scales = keep.tile([P, PAIRS, F, PAIR, F, M_SLOTS, I_CHUNK], U8, align_bytes=64)
 
         identity = keep.tile([P, P], F32)
-        sums = keep.tile([P, F, CIN], F32)
-        result = keep.tile([P, B * T, F], F32)
-        acc = psum.tile([P, HALVES, F, HALF], F32)
-        flipped = psum.tile([P, F, COLS], F32)
+        partial = keep.tile([P, KH, F, CIN], F32)
+        result = keep.tile([P, B, T, F], F32)
+        acc = [psum.tile([P, PAIR, F, M_SLOTS, I_CHUNK], F32, name="acc%d" % k) for k in range(2)]
+        flipped = [psum.tile([P, F, B, T], F32, name="flipped%d" % m) for m in range(KH)]
 
-        for b in range(B):
-            nc.sync.dma_start(
-                out=g_raw[:, b].rearrange("p j t g -> p (j t g)"),
-                in_=grad_out[b].rearrange("(p j) t g -> p (j t g)", j=PACK),
-            )
-        kernel_rows = kernel.rearrange("(p j) i g m n -> p j i (g m n)", j=PACK)
-        for c in range(CHUNKS):
-            nc.sync.dma_start(
-                out=w_raw[c].rearrange("p j i g m n -> p j (i g m n)"),
-                in_=kernel_rows[:, :, c * I_CHUNK : (c + 1) * I_CHUNK, :].rearrange("p j i s -> p j (i s)"),
-            )
+        with tc.manual_schedule():
+            kernel_rows = kernel.rearrange("(p j) i g m n -> p j i (g m n)", j=PACK)
 
-        nc.vector.memset(g_grouped[:, 0, :, :, T - 1, :], 0.0)
-        nc.vector.memset(g_grouped[:, 2, :, :, 0, :], 0.0)
-        for g in range(F):
-            lo, hi = first_out_bin(g), first_out_bin(g) + tap_count(g)
-            for f0, f1 in ((0, lo), (hi, F)):
-                if f0 < f1:
-                    nc.vector.memset(
-                        w_codes[:, g, :, :, f0:f1, :].rearrange("p m h f i -> p (m h) (f i)").bitcast(I32), 0
-                    )
-                    nc.vector.memset(
-                        w_scales[:, g, :, :, f0:f1, :].rearrange("p m h f i -> p (m h) (f i)").bitcast(I32), 0
-                    )
-        make_identity(nc, identity[:])
-
-        for b in range(B):
-            nc.vector.tensor_copy(
-                out=g_grouped[:, 1, :, b].rearrange("p g t j -> p t j g"),
-                in_=g_raw[:, b].rearrange("p j t g -> p t j g"),
-            )
-        nc.vector.tensor_copy(out=g_grouped[:, 0, :, :, 0 : T - 1, :], in_=g_grouped[:, 1, :, :, 1:T, :])
-        nc.vector.tensor_copy(out=g_grouped[:, 2, :, :, 1:T, :], in_=g_grouped[:, 1, :, :, 0 : T - 1, :])
-        for m in (1, 0, 2):
-            nc.vector.quantize_mx(
-                out=g_codes[:, m].rearrange("p g c -> p (g c)").bitcast(E5M2_X4),
-                scales=g_scales[:, m].rearrange("p g c -> p (g c)"),
-                in_=g_grouped[:, m].rearrange("p g b t j -> p (g b t j)"),
-            )
-
-        def quantise_half(g, m, h):
-            for n0 in range(0, tap_count(g), 2):
-                n1 = min(n0 + 2, tap_count(g))
-                f0, f1 = first_out_bin(g) + n0, first_out_bin(g) + n1
-                nc.vector.quantize_mx(
-                    out=w_codes[:, g, m, h, f0:f1, :].rearrange("p f i -> p (f i)").bitcast(E4M3_X4),
-                    scales=w_scales[:, g, m, h, f0:f1, :].rearrange("p f i -> p (f i)"),
-                    in_=w_grouped[(g, h)][:, m, n0:n1].rearrange("p n i j -> p (n i j)"),
+            def load_chunk(c):
+                nc.sync.dma_start(
+                    out=w_raw[c].rearrange("p j i g m n -> p j (i g m n)"),
+                    in_=kernel_rows[:, :, c * I_CHUNK : (c + 1) * I_CHUNK, :].rearrange("p j i s -> p j (i s)"),
                 )
 
-        for c in range(CHUNKS):
-            h = c // CHUNKS_PER_HALF
-            i0 = (c % CHUNKS_PER_HALF) * I_CHUNK
-            for g in VECTOR_BINS:
-                n0, n1 = first_tap(g), first_tap(g) + tap_count(g)
-                nc.vector.tensor_copy(
-                    out=w_grouped[(g, h)][:, :, :, i0 : i0 + I_CHUNK, :].rearrange("p m n i j -> p m i j n"),
-                    in_=w_raw[c][:, :, :, g, :, n0:n1].rearrange("p j i m n -> p m i j n"),
+            load_chunk(0)
+            for b in range(B):
+                nc.sync.dma_start(
+                    out=g_raw[:, b].rearrange("p j s g -> p (j s g)"),
+                    in_=grad_out[b].rearrange("(p j) s g -> p (j s g)", j=PACK),
                 )
-            for g in SCALAR_BINS:
-                n0, n1 = first_tap(g), first_tap(g) + tap_count(g)
-                for m in range(KH):
-                    nc.scalar.copy(
-                        out=w_grouped[(g, h)][:, m, :, i0 : i0 + I_CHUNK, :].rearrange("p n i j -> p i j n"),
-                        in_=w_raw[c][:, :, :, g, m, n0:n1].rearrange("p j i n -> p i j n"),
+            for c in range(1, CHUNKS):
+                load_chunk(c)
+
+            for g in range(F):
+                lo, hi = first_out_bin(g), first_out_bin(g) + tap_count(g)
+                for f0, f1 in ((0, lo), (hi, F)):
+                    if f0 < f1:
+                        for plane in (w_codes, w_scales):
+                            nc.vector.memset(
+                                plane[:, :, g, :, f0:f1].rearrange("p q c f m i -> p q c (f m i)").bitcast(I32), 0
+                            )
+            for k in range(GROUPED_BUFS):
+                nc.gpsimd.memset(w_grouped[k][:, :, KH:M_SLOTS], 0.0)
+            make_identity(nc, identity[:])
+
+            def regroup_chunk(c):
+                grouped = w_grouped[c % GROUPED_BUFS]
+                for g in VECTOR_BINS:
+                    n0, n1 = first_tap(g), first_tap(g) + tap_count(g)
+                    nc.vector.tensor_copy(
+                        out=grouped[:, first_block(g) : first_block(g + 1), 0:KH].rearrange("p n m i j -> p m i j n"),
+                        in_=w_raw[c][:, :, :, g, :, n0:n1].rearrange("p j i m n -> p m i j n"),
                     )
-            if (c + 1) % CHUNKS_PER_HALF == 0:
-                for g in VECTOR_BINS + SCALAR_BINS:
+                for g in SCALAR_BINS:
+                    n0, n1 = first_tap(g), first_tap(g) + tap_count(g)
                     for m in range(KH):
-                        quantise_half(g, m, h)
+                        nc.scalar.copy(
+                            out=grouped[:, first_block(g) : first_block(g + 1), m].rearrange("p n i j -> p i j n"),
+                            in_=w_raw[c][:, :, :, g, m, n0:n1].rearrange("p j i n -> p i j n"),
+                        )
 
-        pairs = [(g, m) for g in VECTOR_BINS + SCALAR_BINS for m in range(KH)]
-        for g, m in pairs:
-            nc.tensor.matmul_mx(
-                out=acc[:].rearrange("p h f i -> p (h f i)"),
-                lhsT=g_codes[:, m, g, :].bitcast(E5M2_X4),
-                lhsT_scale=g_scales[:, m, g, :],
-                rhs=w_codes[:, g, m].rearrange("p h f i -> p (h f i)").bitcast(E4M3_X4),
-                rhs_scale=w_scales[:, g, m].rearrange("p h f i -> p (h f i)"),
-                start=((g, m) == pairs[0]),
-                stop=((g, m) == pairs[-1]),
-            )
+            def quantise_chunk(c, bins):
+                grouped = w_grouped[c % GROUPED_BUFS]
+                for g in bins:
+                    for n0 in range(0, tap_count(g), 2):
+                        n1 = min(n0 + 2, tap_count(g))
+                        f0, f1 = first_out_bin(g) + n0, first_out_bin(g) + n1
+                        nc.vector.quantize_mx(
+                            out=w_codes[:, c // PAIR, g, c % PAIR, f0:f1]
+                            .rearrange("p f m i -> p (f m i)")
+                            .bitcast(E4M3_X4),
+                            scales=w_scales[:, c // PAIR, g, c % PAIR, f0:f1].rearrange("p f m i -> p (f m i)"),
+                            in_=grouped[:, first_block(g) + n0 : first_block(g) + n1].rearrange(
+                                "p n m i j -> p (n m i j)"
+                            ),
+                        )
 
-        for f in range(F):
-            nc.vector.tensor_copy(
-                out=sums[:, f, :].rearrange("p (h i) -> p h i", h=HALVES), in_=acc[:, :, f, :]
-            )
-            nc.tensor.transpose(flipped[:, f, :], sums[:, f, :], identity[:])
-        nc.vector.tensor_copy(out=result[:], in_=flipped[:].rearrange("p f c -> p c f"))
-        nc.sync.dma_start(
-            out=out.rearrange("b i t f -> i b (t f)"),
-            in_=result[:].rearrange("p (b t) f -> p b (t f)", b=B),
-        )
+            def multiply(q, bins):
+                for g in bins:
+                    nc.tensor.matmul_mx(
+                        out=acc[q % 2].rearrange("p c f m i -> p (c f m i)"),
+                        lhsT=g_codes[:, g, :].bitcast(E5M2_X4),
+                        lhsT_scale=g_scales[:, g, :],
+                        rhs=w_codes[:, q, g].rearrange("p c f m i -> p (c f m i)").bitcast(E4M3_X4),
+                        rhs_scale=w_scales[:, q, g].rearrange("p c f m i -> p (c f m i)"),
+                        start=(g == VECTOR_BINS[0]),
+                        stop=(g == SCALAR_BINS[-1]),
+                    )
+
+            def collect(q, m):
+                dst = partial[:, m, :, q * PAIR * I_CHUNK : (q + 1) * PAIR * I_CHUNK].rearrange(
+                    "p f (c i) -> p f c i", c=PAIR
+                )
+                src = acc[q % 2][:, :, :, m, :].rearrange("p c f i -> p f c i")
+                nc.scalar.copy(out=dst, in_=src)
+
+            for c in range(CHUNKS + 1):
+                if c < CHUNKS:
+                    regroup_chunk(c)
+                if c == 0:
+                    for b in range(B):
+                        nc.vector.tensor_copy(
+                            out=g_grouped[:, :, b].rearrange("p g s j -> p s j g"),
+                            in_=g_raw[:, b].rearrange("p j s g -> p s j g"),
+                        )
+                if c >= 1:
+                    quantise_chunk(c - 1, SCALAR_BINS)
+                    if c % PAIR == 0:
+                        multiply(c // PAIR - 1, SCALAR_BINS)
+                if c < CHUNKS:
+                    quantise_chunk(c, VECTOR_BINS)
+                    if c % PAIR == PAIR - 1:
+                        multiply(c // PAIR, VECTOR_BINS)
+                if c == 0:
+                    nc.vector.quantize_mx(
+                        out=g_codes[:].rearrange("p g c -> p (g c)").bitcast(E5M2_X4),
+                        scales=g_scales[:].rearrange("p g c -> p (g c)"),
+                        in_=g_grouped[:].rearrange("p g b s j -> p (g b s j)"),
+                    )
+                if c >= PAIR + 1 and c % PAIR == 1:
+                    for m in range(KH):
+                        collect((c - PAIR - 1) // PAIR, m)
+
+            for m in (1, 0, 2):
+                collect(PAIRS - 1, m)
+                for f in range(F):
+                    nc.tensor.transpose(
+                        flipped[m][:, f].rearrange("p b s -> p (b s)"), partial[:, m, f, :], identity[:]
+                    )
+            for b in range(B):
+                nc.scalar.copy(out=result[:, b], in_=flipped[1][:, :, b].rearrange("p f s -> p s f"))
+            for b in range(B):
+                nc.vector.tensor_tensor(
+                    out=result[:, b, 0 : T - 1],
+                    in0=result[:, b, 0 : T - 1],
+                    in1=flipped[0][:, :, b, 1:T].rearrange("p f s -> p s f"),
+                    op=ADD,
+                )
+            for b in range(B):
+                nc.vector.tensor_tensor(
+                    out=result[:, b, 1:T],
+                    in0=result[:, b, 1:T],
+                    in1=flipped[2][:, :, b, 0 : T - 1].rearrange("p f s -> p s f"),
+                    op=ADD,
+                )
+                nc.sync.dma_start(
+                    out=out[b].rearrange("i t f -> i (t f)"), in_=result[:, b].rearrange("p t f -> p (t f)")
+                )

@@ -8,22 +8,21 @@ U32 = mybir.dt.uint32
 U8 = mybir.dt.uint8
 E4M3_X4 = mybir.dt.float8_e4m3fn_x4
 E5M2_X4 = mybir.dt.float8_e5m2_x4
-ADD = mybir.AluOpType.add
 
 P = 128
 PACK = 4
 B, CIN, COUT, T, F, KH, KW = 2, 128, 512, 64, 4, 3, 3
 COLS = B * T
 
+HALF = 64
+HALVES = CIN // HALF
 I_CHUNK = 16
 CHUNKS = CIN // I_CHUNK
-M_SLOTS = 4
-PAIR = 2
-PAIRS = CHUNKS // PAIR
-GROUPED_BUFS = 4
+CHUNKS_PER_HALF = HALF // I_CHUNK
 
 VECTOR_BINS = (0, 3)
 SCALAR_BINS = (1, 2)
+SCALAR_LAG = 2
 
 FLOPS = 2 * 30 * COUT * CIN * COLS
 BYTES = 2 * B * COUT * T * F + 2 * 30 * COUT * CIN + 4 * B * CIN * T * F
@@ -41,34 +40,33 @@ def first_out_bin(g):
     return g + first_tap(g) - 1
 
 
-def first_block(g):
-    return sum(tap_count(k) for k in range(g))
-
-
 def tile_svconv2d_pa_s_kernel(tc, x, kernel, bias, grad_out, out):
     nc = tc.nc
     with tc.tile_pool(name="keep", bufs=1) as keep, tc.psum_pool(name="psum", bufs=1) as psum:
         g_raw = keep.tile([P, B, PACK, T, F], BF16)
-        g_grouped = keep.tile([P, F, B, T, PACK], BF16, align_bytes=64)
-        g_codes = keep.tile([P, F, COLS], U32, align_bytes=64)
-        g_scales = keep.tile([P, F, COLS], U8, align_bytes=64)
+        g_grouped = keep.tile([P, KH, F, B, T, PACK], BF16, align_bytes=64)
+        g_codes = keep.tile([P, KH, F, COLS], U32, align_bytes=64)
+        g_scales = keep.tile([P, KH, F, COLS], U8, align_bytes=64)
 
         w_raw = [
             keep.tile([P, PACK, I_CHUNK, F, KH, KW], BF16, name="w_raw%d" % c)
             for c in range(CHUNKS)
         ]
-        w_grouped = [
-            keep.tile([P, first_block(F), M_SLOTS, I_CHUNK, PACK], BF16, name="w_grouped%d" % k, align_bytes=64)
-            for k in range(GROUPED_BUFS)
-        ]
-        w_codes = keep.tile([P, PAIRS, F, PAIR, F, M_SLOTS, I_CHUNK], U32, align_bytes=64)
-        w_scales = keep.tile([P, PAIRS, F, PAIR, F, M_SLOTS, I_CHUNK], U8, align_bytes=64)
+        w_grouped = {
+            (g, h): keep.tile(
+                [P, KH, tap_count(g), HALF, PACK], BF16, name="w_grouped%d%d" % (g, h), align_bytes=64
+            )
+            for g in range(F)
+            for h in range(HALVES)
+        }
+        w_codes = keep.tile([P, F, KH, HALVES, F, HALF], U32, align_bytes=64)
+        w_scales = keep.tile([P, F, KH, HALVES, F, HALF], U8, align_bytes=64)
 
         identity = keep.tile([P, P], F32)
-        partial = keep.tile([P, KH, F, CIN], F32)
+        sums = keep.tile([P, F, CIN], F32)
         result = keep.tile([P, B, T, F], F32)
-        acc = [psum.tile([P, PAIR, F, M_SLOTS, I_CHUNK], F32, name="acc%d" % k) for k in range(2)]
-        flipped = [psum.tile([P, F, B, T], F32, name="flipped%d" % m) for m in range(KH)]
+        acc = psum.tile([P, HALVES, F, HALF], F32)
+        flipped = psum.tile([P, F, COLS], F32)
 
         with tc.manual_schedule():
             kernel_rows = kernel.rearrange("(p j) i g m n -> p j i (g m n)", j=PACK)
@@ -82,123 +80,106 @@ def tile_svconv2d_pa_s_kernel(tc, x, kernel, bias, grad_out, out):
             load_chunk(0)
             for b in range(B):
                 nc.sync.dma_start(
-                    out=g_raw[:, b].rearrange("p j s g -> p (j s g)"),
-                    in_=grad_out[b].rearrange("(p j) s g -> p (j s g)", j=PACK),
+                    out=g_raw[:, b].rearrange("p j t g -> p (j t g)"),
+                    in_=grad_out[b].rearrange("(p j) t g -> p (j t g)", j=PACK),
                 )
             for c in range(1, CHUNKS):
                 load_chunk(c)
 
+            nc.vector.memset(g_grouped[:, 0, :, :, T - 1, :], 0.0)
+            nc.vector.memset(g_grouped[:, 2, :, :, 0, :], 0.0)
             for g in range(F):
                 lo, hi = first_out_bin(g), first_out_bin(g) + tap_count(g)
                 for f0, f1 in ((0, lo), (hi, F)):
                     if f0 < f1:
-                        for plane in (w_codes, w_scales):
-                            nc.vector.memset(
-                                plane[:, :, g, :, f0:f1].rearrange("p q c f m i -> p q c (f m i)").bitcast(I32), 0
-                            )
-            for k in range(GROUPED_BUFS):
-                nc.gpsimd.memset(w_grouped[k][:, :, KH:M_SLOTS], 0.0)
+                        nc.vector.memset(
+                            w_codes[:, g, :, :, f0:f1, :].rearrange("p m h f i -> p (m h) (f i)").bitcast(I32), 0
+                        )
+                        nc.vector.memset(
+                            w_scales[:, g, :, :, f0:f1, :].rearrange("p m h f i -> p (m h) (f i)").bitcast(I32), 0
+                        )
             make_identity(nc, identity[:])
 
             def regroup_chunk(c):
-                grouped = w_grouped[c % GROUPED_BUFS]
+                h = c // CHUNKS_PER_HALF
+                i0 = (c % CHUNKS_PER_HALF) * I_CHUNK
                 for g in VECTOR_BINS:
                     n0, n1 = first_tap(g), first_tap(g) + tap_count(g)
                     nc.vector.tensor_copy(
-                        out=grouped[:, first_block(g) : first_block(g + 1), 0:KH].rearrange("p n m i j -> p m i j n"),
+                        out=w_grouped[(g, h)][:, :, :, i0 : i0 + I_CHUNK, :].rearrange("p m n i j -> p m i j n"),
                         in_=w_raw[c][:, :, :, g, :, n0:n1].rearrange("p j i m n -> p m i j n"),
                     )
                 for g in SCALAR_BINS:
                     n0, n1 = first_tap(g), first_tap(g) + tap_count(g)
                     for m in range(KH):
                         nc.scalar.copy(
-                            out=grouped[:, first_block(g) : first_block(g + 1), m].rearrange("p n i j -> p i j n"),
+                            out=w_grouped[(g, h)][:, m, :, i0 : i0 + I_CHUNK, :].rearrange("p n i j -> p i j n"),
                             in_=w_raw[c][:, :, :, g, m, n0:n1].rearrange("p j i n -> p i j n"),
                         )
 
-            def quantise_chunk(c, bins):
-                grouped = w_grouped[c % GROUPED_BUFS]
-                for g in bins:
-                    for n0 in range(0, tap_count(g), 2):
-                        n1 = min(n0 + 2, tap_count(g))
-                        f0, f1 = first_out_bin(g) + n0, first_out_bin(g) + n1
-                        nc.vector.quantize_mx(
-                            out=w_codes[:, c // PAIR, g, c % PAIR, f0:f1]
-                            .rearrange("p f m i -> p (f m i)")
-                            .bitcast(E4M3_X4),
-                            scales=w_scales[:, c // PAIR, g, c % PAIR, f0:f1].rearrange("p f m i -> p (f m i)"),
-                            in_=grouped[:, first_block(g) + n0 : first_block(g) + n1].rearrange(
-                                "p n m i j -> p (n m i j)"
-                            ),
-                        )
-
-            def multiply(q, bins):
-                for g in bins:
-                    nc.tensor.matmul_mx(
-                        out=acc[q % 2].rearrange("p c f m i -> p (c f m i)"),
-                        lhsT=g_codes[:, g, :].bitcast(E5M2_X4),
-                        lhsT_scale=g_scales[:, g, :],
-                        rhs=w_codes[:, q, g].rearrange("p c f m i -> p (c f m i)").bitcast(E4M3_X4),
-                        rhs_scale=w_scales[:, q, g].rearrange("p c f m i -> p (c f m i)"),
-                        start=(g == VECTOR_BINS[0]),
-                        stop=(g == SCALAR_BINS[-1]),
-                    )
-
-            def collect(q, m):
-                dst = partial[:, m, :, q * PAIR * I_CHUNK : (q + 1) * PAIR * I_CHUNK].rearrange(
-                    "p f (c i) -> p f c i", c=PAIR
-                )
-                src = acc[q % 2][:, :, :, m, :].rearrange("p c f i -> p f c i")
-                nc.scalar.copy(out=dst, in_=src)
-
-            for c in range(CHUNKS + 1):
-                if c < CHUNKS:
-                    regroup_chunk(c)
-                if c == 0:
-                    for b in range(B):
-                        nc.vector.tensor_copy(
-                            out=g_grouped[:, :, b].rearrange("p g s j -> p s j g"),
-                            in_=g_raw[:, b].rearrange("p j s g -> p s j g"),
-                        )
-                if c >= 1:
-                    quantise_chunk(c - 1, SCALAR_BINS)
-                    if c % PAIR == 0:
-                        multiply(c // PAIR - 1, SCALAR_BINS)
-                if c < CHUNKS:
-                    quantise_chunk(c, VECTOR_BINS)
-                    if c % PAIR == PAIR - 1:
-                        multiply(c // PAIR, VECTOR_BINS)
-                if c == 0:
+            def quantise_half(g, m, h):
+                for n0 in range(0, tap_count(g), 2):
+                    n1 = min(n0 + 2, tap_count(g))
+                    f0, f1 = first_out_bin(g) + n0, first_out_bin(g) + n1
                     nc.vector.quantize_mx(
-                        out=g_codes[:].rearrange("p g c -> p (g c)").bitcast(E5M2_X4),
-                        scales=g_scales[:].rearrange("p g c -> p (g c)"),
-                        in_=g_grouped[:].rearrange("p g b s j -> p (g b s j)"),
+                        out=w_codes[:, g, m, h, f0:f1, :].rearrange("p f i -> p (f i)").bitcast(E4M3_X4),
+                        scales=w_scales[:, g, m, h, f0:f1, :].rearrange("p f i -> p (f i)"),
+                        in_=w_grouped[(g, h)][:, m, n0:n1].rearrange("p n i j -> p (n i j)"),
                     )
-                if c >= PAIR + 1 and c % PAIR == 1:
-                    for m in range(KH):
-                        collect((c - PAIR - 1) // PAIR, m)
 
-            for m in (1, 0, 2):
-                collect(PAIRS - 1, m)
-                for f in range(F):
-                    nc.tensor.transpose(
-                        flipped[m][:, f].rearrange("p b s -> p (b s)"), partial[:, m, f, :], identity[:]
-                    )
-            for b in range(B):
-                nc.scalar.copy(out=result[:, b], in_=flipped[1][:, :, b].rearrange("p f s -> p s f"))
-            for b in range(B):
-                nc.vector.tensor_tensor(
-                    out=result[:, b, 0 : T - 1],
-                    in0=result[:, b, 0 : T - 1],
-                    in1=flipped[0][:, :, b, 1:T].rearrange("p f s -> p s f"),
-                    op=ADD,
+            pairs = [(g, m) for g in VECTOR_BINS + SCALAR_BINS for m in range(KH)]
+
+            def multiply(g, m):
+                nc.tensor.matmul_mx(
+                    out=acc[:].rearrange("p h f i -> p (h f i)"),
+                    lhsT=g_codes[:, m, g, :].bitcast(E5M2_X4),
+                    lhsT_scale=g_scales[:, m, g, :],
+                    rhs=w_codes[:, g, m].rearrange("p h f i -> p (h f i)").bitcast(E4M3_X4),
+                    rhs_scale=w_scales[:, g, m].rearrange("p h f i -> p (h f i)"),
+                    start=((g, m) == pairs[0]),
+                    stop=((g, m) == pairs[-1]),
                 )
+
+            def quantise_bins(bins, h):
+                for g in bins:
+                    for m in range(KH):
+                        quantise_half(g, m, h)
+                        if h == HALVES - 1:
+                            multiply(g, m)
+
+            regroup_chunk(0)
+
             for b in range(B):
-                nc.vector.tensor_tensor(
-                    out=result[:, b, 1:T],
-                    in0=result[:, b, 1:T],
-                    in1=flipped[2][:, :, b, 0 : T - 1].rearrange("p f s -> p s f"),
-                    op=ADD,
+                nc.vector.tensor_copy(
+                    out=g_grouped[:, 1, :, b].rearrange("p g t j -> p t j g"),
+                    in_=g_raw[:, b].rearrange("p j t g -> p t j g"),
+                )
+            nc.vector.tensor_copy(out=g_grouped[:, 0, :, :, 0 : T - 1, :], in_=g_grouped[:, 1, :, :, 1:T, :])
+            nc.vector.tensor_copy(out=g_grouped[:, 2, :, :, 1:T, :], in_=g_grouped[:, 1, :, :, 0 : T - 1, :])
+            for m in (1, 0, 2):
+                nc.vector.quantize_mx(
+                    out=g_codes[:, m].rearrange("p g c -> p (g c)").bitcast(E5M2_X4),
+                    scales=g_scales[:, m].rearrange("p g c -> p (g c)"),
+                    in_=g_grouped[:, m].rearrange("p g b t j -> p (g b t j)"),
+                )
+
+            for c in range(1, CHUNKS):
+                regroup_chunk(c)
+                h, place = divmod(c, CHUNKS_PER_HALF)
+                if place == CHUNKS_PER_HALF - 1:
+                    quantise_bins(VECTOR_BINS, h)
+                if place == SCALAR_LAG - 1 and h > 0:
+                    quantise_bins(SCALAR_BINS, h - 1)
+            quantise_bins(SCALAR_BINS, HALVES - 1)
+
+            for f in range(F):
+                nc.vector.tensor_copy(
+                    out=sums[:, f, :].rearrange("p (h i) -> p h i", h=HALVES), in_=acc[:, :, f, :]
+                )
+                nc.tensor.transpose(flipped[:, f, :], sums[:, f, :], identity[:])
+            for b in range(B):
+                nc.vector.tensor_copy(
+                    out=result[:, b], in_=flipped[:, :, b * T : (b + 1) * T].rearrange("p f t -> p t f")
                 )
                 nc.sync.dma_start(
                     out=out[b].rearrange("i t f -> i (t f)"), in_=result[:, b].rearrange("p t f -> p (t f)")

@@ -13,16 +13,17 @@ P = 128
 PACK = 4
 B, CIN, COUT, T, F, KH, KW = 2, 128, 512, 64, 4, 3, 3
 COLS = B * T
+TH = T // 2
+BLOCK = B * TH
 
 HALF = 64
 HALVES = CIN // HALF
-I_CHUNK = 16
-CHUNKS = CIN // I_CHUNK
-CHUNKS_PER_HALF = HALF // I_CHUNK
+CHUNK_SIZES = (16, 16, 32, 32, 16, 16)
+CHUNK_STARTS = tuple(sum(CHUNK_SIZES[:c]) for c in range(len(CHUNK_SIZES)))
+CHUNKS = len(CHUNK_SIZES)
+LAST = CHUNKS - 1
 
-VECTOR_BINS = (0, 3)
-SCALAR_BINS = (1, 2)
-SCALAR_LAG = 2
+VECTOR_SHARE = ((0, 0), (1, 0), (2, 0), (2, 3), (3, 0), (3, 3), (4, 0), (4, 3))
 
 FLOPS = 2 * 30 * COUT * CIN * COLS
 BYTES = 2 * B * COUT * T * F + 2 * 30 * COUT * CIN + 4 * B * CIN * T * F
@@ -43,13 +44,13 @@ def first_out_bin(g):
 def tile_svconv2d_pa_s_kernel(tc, x, kernel, bias, grad_out, out):
     nc = tc.nc
     with tc.tile_pool(name="keep", bufs=1) as keep, tc.psum_pool(name="psum", bufs=1) as psum:
-        g_raw = keep.tile([P, B, PACK, T, F], BF16)
-        g_grouped = keep.tile([P, KH, F, B, T, PACK], BF16, align_bytes=64)
-        g_codes = keep.tile([P, KH, F, COLS], U32, align_bytes=64)
-        g_scales = keep.tile([P, KH, F, COLS], U8, align_bytes=64)
+        g_raw = keep.tile([P, B, PACK, TH, 2, F], BF16)
+        g_grouped = keep.tile([P, F, 4, B, TH, PACK], BF16, align_bytes=64)
+        g_codes = keep.tile([P, F, 4, BLOCK], U32, align_bytes=64)
+        g_scales = keep.tile([P, F, 4, BLOCK], U8, align_bytes=64)
 
         w_raw = [
-            keep.tile([P, PACK, I_CHUNK, F, KH, KW], BF16, name="w_raw%d" % c)
+            keep.tile([P, PACK, CHUNK_SIZES[c], F, KH, KW], BF16, name="w_raw%d" % c)
             for c in range(CHUNKS)
         ]
         w_grouped = {
@@ -64,58 +65,53 @@ def tile_svconv2d_pa_s_kernel(tc, x, kernel, bias, grad_out, out):
 
         identity = keep.tile([P, P], F32)
         sums = keep.tile([P, F, CIN], F32)
-        result = keep.tile([P, B, T, F], F32)
+        result = keep.tile([P, B, TH, 2, F], F32)
         acc = psum.tile([P, HALVES, F, HALF], F32)
-        flipped = psum.tile([P, F, COLS], F32)
+        flipped = psum.tile([P, F, 2, B, TH], F32)
 
         with tc.manual_schedule():
             kernel_rows = kernel.rearrange("(p j) i g m n -> p j i (g m n)", j=PACK)
 
             def load_chunk(c):
+                i0 = CHUNK_STARTS[c]
                 nc.sync.dma_start(
                     out=w_raw[c].rearrange("p j i g m n -> p j (i g m n)"),
-                    in_=kernel_rows[:, :, c * I_CHUNK : (c + 1) * I_CHUNK, :].rearrange("p j i s -> p j (i s)"),
+                    in_=kernel_rows[:, :, i0 : i0 + CHUNK_SIZES[c], :].rearrange("p j i s -> p j (i s)"),
                 )
 
             load_chunk(0)
-            for b in range(B):
-                nc.sync.dma_start(
-                    out=g_raw[:, b].rearrange("p j t g -> p (j t g)"),
-                    in_=grad_out[b].rearrange("(p j) t g -> p (j t g)", j=PACK),
-                )
+            nc.sync.dma_start(
+                out=g_raw.rearrange("p b j t e g -> p b (j t e g)"),
+                in_=grad_out.rearrange("b (p j) t g -> p b (j t g)", j=PACK),
+            )
             for c in range(1, CHUNKS):
                 load_chunk(c)
 
-            nc.vector.memset(g_grouped[:, 0, :, :, T - 1, :], 0.0)
-            nc.vector.memset(g_grouped[:, 2, :, :, 0, :], 0.0)
+            nc.vector.memset(g_grouped[:, :, 0, :, 0, :], 0.0)
+            nc.vector.memset(g_grouped[:, :, 3, :, TH - 1, :], 0.0)
+            make_identity(nc, identity[:])
             for g in range(F):
                 lo, hi = first_out_bin(g), first_out_bin(g) + tap_count(g)
                 for f0, f1 in ((0, lo), (hi, F)):
                     if f0 < f1:
-                        nc.vector.memset(
-                            w_codes[:, g, :, :, f0:f1, :].rearrange("p m h f i -> p (m h) (f i)").bitcast(I32), 0
-                        )
+                        empty_codes = w_codes[:, g, :, :, f0:f1, :].rearrange("p m h f i -> p (m h) (f i)")
+                        if g in (1, 2):
+                            nc.gpsimd.memset(empty_codes.bitcast(F32), 0.0)
+                        else:
+                            nc.vector.memset(empty_codes.bitcast(I32), 0)
                         nc.vector.memset(
                             w_scales[:, g, :, :, f0:f1, :].rearrange("p m h f i -> p (m h) (f i)").bitcast(I32), 0
                         )
-            make_identity(nc, identity[:])
 
-            def regroup_chunk(c):
-                h = c // CHUNKS_PER_HALF
-                i0 = (c % CHUNKS_PER_HALF) * I_CHUNK
-                for g in VECTOR_BINS:
-                    n0, n1 = first_tap(g), first_tap(g) + tap_count(g)
-                    nc.vector.tensor_copy(
-                        out=w_grouped[(g, h)][:, :, :, i0 : i0 + I_CHUNK, :].rearrange("p m n i j -> p m i j n"),
-                        in_=w_raw[c][:, :, :, g, :, n0:n1].rearrange("p j i m n -> p m i j n"),
-                    )
-                for g in SCALAR_BINS:
-                    n0, n1 = first_tap(g), first_tap(g) + tap_count(g)
-                    for m in range(KH):
-                        nc.scalar.copy(
-                            out=w_grouped[(g, h)][:, m, :, i0 : i0 + I_CHUNK, :].rearrange("p n i j -> p i j n"),
-                            in_=w_raw[c][:, :, :, g, m, n0:n1].rearrange("p j i n -> p i j n"),
-                        )
+            def regroup(c, g, m0, m1):
+                h, i0 = divmod(CHUNK_STARTS[c], HALF)
+                n0, n1 = first_tap(g), first_tap(g) + tap_count(g)
+                dst = w_grouped[(g, h)][:, m0:m1, :, i0 : i0 + CHUNK_SIZES[c], :].rearrange("p m n i j -> p m i j n")
+                src = w_raw[c][:, :, :, g, m0:m1, n0:n1].rearrange("p j i m n -> p m i j n")
+                if (c, g) in VECTOR_SHARE:
+                    nc.vector.tensor_copy(out=dst, in_=src)
+                else:
+                    nc.scalar.copy(out=dst, in_=src)
 
             def quantise_half(g, m, h):
                 for n0 in range(0, tap_count(g), 2):
@@ -127,60 +123,61 @@ def tile_svconv2d_pa_s_kernel(tc, x, kernel, bias, grad_out, out):
                         in_=w_grouped[(g, h)][:, m, n0:n1].rearrange("p n i j -> p (n i j)"),
                     )
 
-            pairs = [(g, m) for g in VECTOR_BINS + SCALAR_BINS for m in range(KH)]
+            pairs = [(g, m) for g in (1, 2, 0, 3) for m in range(KH)]
 
             def multiply(g, m):
                 nc.tensor.matmul_mx(
                     out=acc[:].rearrange("p h f i -> p (h f i)"),
-                    lhsT=g_codes[:, m, g, :].bitcast(E5M2_X4),
-                    lhsT_scale=g_scales[:, m, g, :],
+                    lhsT=g_codes[:, g, 2 - m : 4 - m, :].rearrange("p k c -> p (k c)").bitcast(E5M2_X4),
+                    lhsT_scale=g_scales[:, g, 2 - m : 4 - m, :].rearrange("p k c -> p (k c)"),
                     rhs=w_codes[:, g, m].rearrange("p h f i -> p (h f i)").bitcast(E4M3_X4),
                     rhs_scale=w_scales[:, g, m].rearrange("p h f i -> p (h f i)"),
                     start=((g, m) == pairs[0]),
                     stop=((g, m) == pairs[-1]),
                 )
 
-            def quantise_bins(bins, h):
-                for g in bins:
-                    for m in range(KH):
-                        quantise_half(g, m, h)
-                        if h == HALVES - 1:
-                            multiply(g, m)
+            def regroup_chunk(c):
+                for g in (0, 3, 1, 2):
+                    regroup(c, g, 0, KH)
 
             regroup_chunk(0)
 
-            for b in range(B):
+            for e in range(2):
                 nc.vector.tensor_copy(
-                    out=g_grouped[:, 1, :, b].rearrange("p g t j -> p t j g"),
-                    in_=g_raw[:, b].rearrange("p j t g -> p t j g"),
+                    out=g_grouped[:, :, 1 + e].rearrange("p g b t j -> p b t j g"),
+                    in_=g_raw[:, :, :, :, e, :].rearrange("p b j t g -> p b t j g"),
                 )
-            nc.vector.tensor_copy(out=g_grouped[:, 0, :, :, 0 : T - 1, :], in_=g_grouped[:, 1, :, :, 1:T, :])
-            nc.vector.tensor_copy(out=g_grouped[:, 2, :, :, 1:T, :], in_=g_grouped[:, 1, :, :, 0 : T - 1, :])
-            for m in (1, 0, 2):
-                nc.vector.quantize_mx(
-                    out=g_codes[:, m].rearrange("p g c -> p (g c)").bitcast(E5M2_X4),
-                    scales=g_scales[:, m].rearrange("p g c -> p (g c)"),
-                    in_=g_grouped[:, m].rearrange("p g b t j -> p (g b t j)"),
-                )
-
-            for c in range(1, CHUNKS):
-                regroup_chunk(c)
-                h, place = divmod(c, CHUNKS_PER_HALF)
-                if place == CHUNKS_PER_HALF - 1:
-                    quantise_bins(VECTOR_BINS, h)
-                if place == SCALAR_LAG - 1 and h > 0:
-                    quantise_bins(SCALAR_BINS, h - 1)
-            quantise_bins(SCALAR_BINS, HALVES - 1)
+            nc.vector.tensor_copy(out=g_grouped[:, :, 3, :, 0 : TH - 1, :], in_=g_grouped[:, :, 1, :, 1:TH, :])
+            nc.vector.tensor_copy(out=g_grouped[:, :, 0, :, 1:TH, :], in_=g_grouped[:, :, 2, :, 0 : TH - 1, :])
+            regroup_chunk(1)
+            nc.vector.quantize_mx(
+                out=g_codes.rearrange("p g k c -> p (g k c)").bitcast(E5M2_X4),
+                scales=g_scales.rearrange("p g k c -> p (g k c)"),
+                in_=g_grouped.rearrange("p g k b t j -> p (g k b t j)"),
+            )
+            regroup_chunk(2)
+            for g in (0, 3):
+                for m in range(KH):
+                    quantise_half(g, m, 0)
+            regroup_chunk(3)
+            for g in (1, 2):
+                for m in range(KH):
+                    quantise_half(g, m, 0)
+            regroup_chunk(4)
+            for g, m in pairs:
+                regroup(LAST, g, m, m + 1)
+                quantise_half(g, m, 1)
+                multiply(g, m)
 
             for f in range(F):
                 nc.vector.tensor_copy(
                     out=sums[:, f, :].rearrange("p (h i) -> p h i", h=HALVES), in_=acc[:, :, f, :]
                 )
-                nc.tensor.transpose(flipped[:, f, :], sums[:, f, :], identity[:])
+                nc.tensor.transpose(flipped[:, f].rearrange("p e b t -> p (e b t)"), sums[:, f, :], identity[:])
             for b in range(B):
                 nc.vector.tensor_copy(
-                    out=result[:, b], in_=flipped[:, :, b * T : (b + 1) * T].rearrange("p f t -> p t f")
+                    out=result[:, b], in_=flipped[:, :, :, b, :].rearrange("p f e t -> p t e f")
                 )
                 nc.sync.dma_start(
-                    out=out[b].rearrange("i t f -> i (t f)"), in_=result[:, b].rearrange("p t f -> p (t f)")
+                    out=out[b].rearrange("i t f -> i (t f)"), in_=result[:, b].rearrange("p t e f -> p (t e f)")
                 )

@@ -18,12 +18,12 @@ BLOCK = B * TH
 
 HALF = 64
 HALVES = CIN // HALF
-CHUNK_SIZES = (16, 16, 32, 32, 16, 16)
+CHUNK_SIZES = (16, 16, 32, 32, 32)
 CHUNK_STARTS = tuple(sum(CHUNK_SIZES[:c]) for c in range(len(CHUNK_SIZES)))
 CHUNKS = len(CHUNK_SIZES)
 LAST = CHUNKS - 1
 
-VECTOR_SHARE = ((0, 0), (1, 0), (2, 0), (2, 3), (3, 0), (3, 3), (4, 0), (4, 3))
+VECTOR_SHARE = ((0, 0), (0, 3), (0, 2), (2, 0), (2, 3), (3, 0), (4, 0), (4, 3))
 
 FLOPS = 2 * 30 * COUT * CIN * COLS
 BYTES = 2 * B * COUT * T * F + 2 * 30 * COUT * CIN + 4 * B * CIN * T * F
@@ -50,7 +50,7 @@ def tile_svconv2d_pa_s_kernel(tc, x, kernel, bias, grad_out, out):
         g_scales = keep.tile([P, F, 4, BLOCK], U8, align_bytes=64)
 
         w_raw = [
-            keep.tile([P, PACK, CHUNK_SIZES[c], F, KH, KW], BF16, name="w_raw%d" % c)
+            keep.tile([P, PACK, CHUNK_SIZES[c] * F * KH * KW], BF16, name="w_raw%d" % c)
             for c in range(CHUNKS)
         ]
         w_grouped = {
@@ -68,6 +68,7 @@ def tile_svconv2d_pa_s_kernel(tc, x, kernel, bias, grad_out, out):
         result = keep.tile([P, B, TH, 2, F], F32)
         acc = psum.tile([P, HALVES, F, HALF], F32)
         flipped = psum.tile([P, F, 2, B, TH], F32)
+        idle_bank = psum.tile([P, 512], F32)
 
         with tc.manual_schedule():
             kernel_rows = kernel.rearrange("(p j) i g m n -> p j i (g m n)", j=PACK)
@@ -75,7 +76,7 @@ def tile_svconv2d_pa_s_kernel(tc, x, kernel, bias, grad_out, out):
             def load_chunk(c):
                 i0 = CHUNK_STARTS[c]
                 nc.sync.dma_start(
-                    out=w_raw[c].rearrange("p j i g m n -> p j (i g m n)"),
+                    out=w_raw[c][:],
                     in_=kernel_rows[:, :, i0 : i0 + CHUNK_SIZES[c], :].rearrange("p j i s -> p j (i s)"),
                 )
 
@@ -107,7 +108,8 @@ def tile_svconv2d_pa_s_kernel(tc, x, kernel, bias, grad_out, out):
                 h, i0 = divmod(CHUNK_STARTS[c], HALF)
                 n0, n1 = first_tap(g), first_tap(g) + tap_count(g)
                 dst = w_grouped[(g, h)][:, m0:m1, :, i0 : i0 + CHUNK_SIZES[c], :].rearrange("p m n i j -> p m i j n")
-                src = w_raw[c][:, :, :, g, m0:m1, n0:n1].rearrange("p j i m n -> p m i j n")
+                taps = w_raw[c].rearrange("p j (i g m n) -> p j i g m n", g=F, m=KH, n=KW)
+                src = taps[:, :, :, g, m0:m1, n0:n1].rearrange("p j i m n -> p m i j n")
                 if (c, g) in VECTOR_SHARE:
                     nc.vector.tensor_copy(out=dst, in_=src)
                 else:
@@ -123,7 +125,7 @@ def tile_svconv2d_pa_s_kernel(tc, x, kernel, bias, grad_out, out):
                         in_=w_grouped[(g, h)][:, m, n0:n1].rearrange("p n i j -> p (n i j)"),
                     )
 
-            pairs = [(g, m) for g in (1, 2, 0, 3) for m in range(KH)]
+            pairs = [(g, m) for g in (0, 3, 1, 2) for m in range(KH)]
 
             def multiply(g, m):
                 nc.tensor.matmul_mx(
@@ -136,38 +138,55 @@ def tile_svconv2d_pa_s_kernel(tc, x, kernel, bias, grad_out, out):
                     stop=((g, m) == pairs[-1]),
                 )
 
-            def regroup_chunk(c):
-                for g in (0, 3, 1, 2):
-                    regroup(c, g, 0, KH)
+            def regroup_grad(e):
+                dst = g_grouped[:, :, 1 + e].rearrange("p g b t j -> p b t j g")
+                src = g_raw[:, :, :, :, e, :].rearrange("p b j t g -> p b t j g")
+                if e == 0:
+                    nc.vector.tensor_copy(out=dst, in_=src)
+                else:
+                    nc.scalar.copy(out=dst, in_=src)
 
-            regroup_chunk(0)
+            def quantise_bin(g, h):
+                for m in range(KH):
+                    quantise_half(g, m, h)
+                    if h == HALVES - 1:
+                        multiply(g, m)
 
-            for e in range(2):
-                nc.vector.tensor_copy(
-                    out=g_grouped[:, :, 1 + e].rearrange("p g b t j -> p b t j g"),
-                    in_=g_raw[:, :, :, :, e, :].rearrange("p b j t g -> p b t j g"),
-                )
+            def keep_clock_up(c):
+                for j in range(3):
+                    nc.tensor.matmul(
+                        out=idle_bank[:, 0:P],
+                        lhsT=identity[:],
+                        rhs=w_raw[c][:, j, 0 : 2 * P].bitcast(F32),
+                        start=True,
+                        stop=True,
+                    )
+
+            for g in (0, 1, 3, 2):
+                regroup(0, g, 0, KH)
+            regroup_grad(0)
+            regroup_grad(1)
             nc.vector.tensor_copy(out=g_grouped[:, :, 3, :, 0 : TH - 1, :], in_=g_grouped[:, :, 1, :, 1:TH, :])
             nc.vector.tensor_copy(out=g_grouped[:, :, 0, :, 1:TH, :], in_=g_grouped[:, :, 2, :, 0 : TH - 1, :])
-            regroup_chunk(1)
+            for g in (1, 2, 0, 3):
+                regroup(1, g, 0, KH)
             nc.vector.quantize_mx(
                 out=g_codes.rearrange("p g k c -> p (g k c)").bitcast(E5M2_X4),
                 scales=g_scales.rearrange("p g k c -> p (g k c)"),
                 in_=g_grouped.rearrange("p g k b t j -> p (g k b t j)"),
             )
-            regroup_chunk(2)
-            for g in (0, 3):
-                for m in range(KH):
-                    quantise_half(g, m, 0)
-            regroup_chunk(3)
-            for g in (1, 2):
-                for m in range(KH):
-                    quantise_half(g, m, 0)
-            regroup_chunk(4)
-            for g, m in pairs:
-                regroup(LAST, g, m, m + 1)
-                quantise_half(g, m, 1)
-                multiply(g, m)
+            for g in (0, 1, 3, 2):
+                regroup(2, g, 0, KH)
+            for g in (0, 1, 2, 3):
+                quantise_bin(g, 0)
+            keep_clock_up(3)
+            for g in (1, 2, 0, 3):
+                regroup(3, g, 0, KH)
+            keep_clock_up(4)
+            for g in (0, 3, 1, 2):
+                regroup(4, g, 0, KH)
+            for g in (0, 3, 1, 2):
+                quantise_bin(g, 1)
 
             for f in range(F):
                 nc.vector.tensor_copy(

@@ -23,7 +23,9 @@ CHUNK_STARTS = tuple(sum(CHUNK_SIZES[:c]) for c in range(len(CHUNK_SIZES)))
 CHUNKS = len(CHUNK_SIZES)
 LAST = CHUNKS - 1
 
-VECTOR_SHARE = ((0, 0), (0, 3), (0, 2), (2, 0), (2, 3), (3, 0), (4, 0), (4, 3))
+TAPS = F * KH * KW
+RUN = 4
+SCALAR_RUNS = (2, 7)
 
 FLOPS = 2 * 30 * COUT * CIN * COLS
 BYTES = 2 * B * COUT * T * F + 2 * 30 * COUT * CIN + 4 * B * CIN * T * F
@@ -53,13 +55,9 @@ def tile_svconv2d_pa_s_kernel(tc, x, kernel, bias, grad_out, out):
             keep.tile([P, PACK, CHUNK_SIZES[c] * F * KH * KW], BF16, name="w_raw%d" % c)
             for c in range(CHUNKS)
         ]
-        w_grouped = {
-            (g, h): keep.tile(
-                [P, KH, tap_count(g), HALF, PACK], BF16, name="w_grouped%d%d" % (g, h), align_bytes=64
-            )
-            for g in range(F)
-            for h in range(HALVES)
-        }
+        w_grouped = [
+            keep.tile([P, TAPS, HALF, PACK], BF16, name="w_grouped%d" % h, align_bytes=64) for h in range(HALVES)
+        ]
         w_codes = keep.tile([P, F, KH, HALVES, F, HALF], U32, align_bytes=64)
         w_scales = keep.tile([P, F, KH, HALVES, F, HALF], U8, align_bytes=64)
 
@@ -104,28 +102,48 @@ def tile_svconv2d_pa_s_kernel(tc, x, kernel, bias, grad_out, out):
                             w_scales[:, g, :, :, f0:f1, :].rearrange("p m h f i -> p (m h) (f i)").bitcast(I32), 0
                         )
 
-            def regroup(c, g, m0, m1):
+            def views(c):
                 h, i0 = divmod(CHUNK_STARTS[c], HALF)
-                n0, n1 = first_tap(g), first_tap(g) + tap_count(g)
-                dst = w_grouped[(g, h)][:, m0:m1, :, i0 : i0 + CHUNK_SIZES[c], :].rearrange("p m n i j -> p m i j n")
-                taps = w_raw[c].rearrange("p j (i g m n) -> p j i g m n", g=F, m=KH, n=KW)
-                src = taps[:, :, :, g, m0:m1, n0:n1].rearrange("p j i m n -> p m i j n")
-                if (c, g) in VECTOR_SHARE:
-                    nc.vector.tensor_copy(out=dst, in_=src)
-                else:
-                    nc.scalar.copy(out=dst, in_=src)
+                src = w_raw[c].rearrange("p j (i s) -> p j i s", s=TAPS)
+                dst = w_grouped[h][:, :, i0 : i0 + CHUNK_SIZES[c], :]
+                return src, dst
+
+            def scalar_runs(c, k0, k1):
+                src, dst = views(c)
+                nc.scalar.copy(
+                    out=dst[:, RUN * k0 : RUN * k1].rearrange("p (k q) i j -> p k i j q", q=RUN),
+                    in_=src[:, :, :, RUN * k0 : RUN * k1].rearrange("p j i (k q) -> p k i j q", q=RUN),
+                )
+
+            def vector_pairs(c, s0, n0):
+                src, dst = views(c)
+                nc.vector.tensor_copy(
+                    out=dst[:, s0 : s0 + 2 * KW].rearrange("p (m n) i j -> p m i j n", n=KW)[:, :, :, :, n0 : n0 + 2],
+                    in_=src[:, :, :, s0 : s0 + 2 * KW].rearrange("p j i (m n) -> p m i j n", n=KW)[:, :, :, :, n0 : n0 + 2],
+                )
+
+            def vector_singles(c):
+                src, dst = views(c)
+                nc.vector.tensor_copy(
+                    out=dst[:, 7:TAPS:21],
+                    in_=src[:, :, :, 7:TAPS:21].rearrange("p j i x -> p x i j"),
+                )
 
             def quantise_half(g, m, h):
+                s0 = (g * KH + m) * KW + first_tap(g)
                 for n0 in range(0, tap_count(g), 2):
                     n1 = min(n0 + 2, tap_count(g))
                     f0, f1 = first_out_bin(g) + n0, first_out_bin(g) + n1
                     nc.vector.quantize_mx(
                         out=w_codes[:, g, m, h, f0:f1, :].rearrange("p f i -> p (f i)").bitcast(E4M3_X4),
                         scales=w_scales[:, g, m, h, f0:f1, :].rearrange("p f i -> p (f i)"),
-                        in_=w_grouped[(g, h)][:, m, n0:n1].rearrange("p n i j -> p (n i j)"),
+                        in_=w_grouped[h][:, s0 + n0 : s0 + n1].rearrange("p n i j -> p (n i j)"),
                     )
 
-            pairs = [(g, m) for g in (0, 3, 1, 2) for m in range(KH)]
+            own = [(0, 0), (0, 1), (3, 1), (3, 2)]
+            early = [(0, 2), (1, 0), (1, 1)]
+            late = [(1, 2), (2, 0), (2, 1), (2, 2), (3, 0)]
+            pairs = own + early + late
 
             def multiply(g, m):
                 nc.tensor.matmul_mx(
@@ -162,31 +180,47 @@ def tile_svconv2d_pa_s_kernel(tc, x, kernel, bias, grad_out, out):
                         stop=True,
                     )
 
-            for g in (0, 1, 3, 2):
-                regroup(0, g, 0, KH)
+            def vector_share(c):
+                vector_pairs(c, 0, 1)
+                vector_pairs(c, TAPS - 2 * KW, 0)
+                vector_singles(c)
+
+            def scalar_share(c):
+                scalar_runs(c, 2, 4)
+                scalar_runs(c, 4, 7)
+
+            def quantise(units, h):
+                for g, m in units:
+                    quantise_half(g, m, h)
+                    if h == HALVES - 1:
+                        multiply(g, m)
+
+            vector_share(0)
+            scalar_share(0)
             regroup_grad(0)
             regroup_grad(1)
             nc.vector.tensor_copy(out=g_grouped[:, :, 3, :, 0 : TH - 1, :], in_=g_grouped[:, :, 1, :, 1:TH, :])
             nc.vector.tensor_copy(out=g_grouped[:, :, 0, :, 1:TH, :], in_=g_grouped[:, :, 2, :, 0 : TH - 1, :])
-            for g in (1, 2, 0, 3):
-                regroup(1, g, 0, KH)
+            scalar_share(1)
             nc.vector.quantize_mx(
                 out=g_codes.rearrange("p g k c -> p (g k c)").bitcast(E5M2_X4),
                 scales=g_scales.rearrange("p g k c -> p (g k c)"),
                 in_=g_grouped.rearrange("p g k b t j -> p (g k b t j)"),
             )
-            for g in (0, 1, 3, 2):
-                regroup(2, g, 0, KH)
-            for g in (0, 1, 2, 3):
-                quantise_bin(g, 0)
+            vector_share(1)
+            vector_share(2)
+            scalar_share(2)
+            quantise(own, 0)
+            quantise(early, 0)
             keep_clock_up(3)
-            for g in (1, 2, 0, 3):
-                regroup(3, g, 0, KH)
+            vector_share(3)
+            scalar_share(3)
+            quantise(late, 0)
             keep_clock_up(4)
-            for g in (0, 3, 1, 2):
-                regroup(4, g, 0, KH)
-            for g in (0, 3, 1, 2):
-                quantise_bin(g, 1)
+            vector_share(4)
+            for k in range(2, 7):
+                scalar_runs(4, k, k + 1)
+            quantise(pairs, 1)
 
             for f in range(F):
                 nc.vector.tensor_copy(

@@ -25,6 +25,7 @@ LAST = CHUNKS - 1
 
 TAPS = F * KH * KW
 RUN = 4
+VECTOR_TAKES_RUN_6 = (2, 3)
 SCALAR_RUNS = (2, 7)
 
 FLOPS = 2 * 30 * COUT * CIN * COLS
@@ -180,14 +181,23 @@ def tile_svconv2d_pa_s_kernel(tc, x, kernel, bias, grad_out, out):
                         stop=True,
                     )
 
+            def vector_run(c, k):
+                src, dst = views(c)
+                nc.vector.tensor_copy(
+                    out=dst[:, RUN * k : RUN * (k + 1)].rearrange("p q i j -> p i j q"),
+                    in_=src[:, :, :, RUN * k : RUN * (k + 1)].rearrange("p j i q -> p i j q"),
+                )
+
             def vector_share(c):
                 vector_pairs(c, 0, 1)
                 vector_pairs(c, TAPS - 2 * KW, 0)
                 vector_singles(c)
+                if c in VECTOR_TAKES_RUN_6:
+                    vector_run(c, 6)
 
             def scalar_share(c):
                 scalar_runs(c, 2, 4)
-                scalar_runs(c, 4, 7)
+                scalar_runs(c, 4, 6 if c in VECTOR_TAKES_RUN_6 else 7)
 
             def quantise(units, h):
                 for g, m in units:

@@ -144,7 +144,7 @@ def tile_svconv2d_pa_s_kernel(tc, x, kernel, bias, grad_out, out):
             own = [(0, 0), (0, 1), (3, 1), (3, 2)]
             early = [(0, 2), (1, 0), (1, 1)]
             late = [(1, 2), (2, 0), (2, 1), (2, 2), (3, 0)]
-            pairs = own + early + late
+            pairs = own[0:2] + early[0:1] + own[2:4] + early[1:3] + late
 
             def multiply(g, m):
                 nc.tensor.matmul_mx(
@@ -171,8 +171,8 @@ def tile_svconv2d_pa_s_kernel(tc, x, kernel, bias, grad_out, out):
                     if h == HALVES - 1:
                         multiply(g, m)
 
-            def keep_clock_up(c):
-                for j in range(3):
+            def keep_clock_up(c, products):
+                for j in range(products):
                     nc.tensor.matmul(
                         out=idle_bank[:, 0:P],
                         lhsT=identity[:],
@@ -222,15 +222,18 @@ def tile_svconv2d_pa_s_kernel(tc, x, kernel, bias, grad_out, out):
             scalar_share(2)
             quantise(own, 0)
             quantise(early, 0)
-            keep_clock_up(3)
+            keep_clock_up(3, 3)
             vector_share(3)
             scalar_share(3)
             quantise(late, 0)
-            keep_clock_up(4)
-            vector_share(4)
+            keep_clock_up(4, 2)
             for k in range(2, 7):
                 scalar_runs(4, k, k + 1)
-            quantise(pairs, 1)
+            vector_pairs(4, 0, 1)
+            vector_singles(4)
+            quantise(pairs[0:2], 1)
+            vector_pairs(4, TAPS - 2 * KW, 0)
+            quantise(pairs[2:], 1)
 
             for f in range(F):
                 nc.vector.tensor_copy(

@@ -18,14 +18,14 @@ BLOCK = B * TH
 
 HALF = 64
 HALVES = CIN // HALF
-CHUNK_SIZES = (16, 16, 32, 32, 32)
+CHUNK_SIZES = (32, 32, 32, 32)
 CHUNK_STARTS = tuple(sum(CHUNK_SIZES[:c]) for c in range(len(CHUNK_SIZES)))
 CHUNKS = len(CHUNK_SIZES)
 LAST = CHUNKS - 1
 
 TAPS = F * KH * KW
 RUN = 4
-VECTOR_TAKES_RUN_6 = (2, 3)
+VECTOR_TAKES_RUN_6 = (1, 2)
 SCALAR_RUNS = (2, 7)
 
 FLOPS = 2 * 30 * COUT * CIN * COLS
@@ -79,12 +79,11 @@ def tile_svconv2d_pa_s_kernel(tc, x, kernel, bias, grad_out, out):
                     in_=kernel_rows[:, :, i0 : i0 + CHUNK_SIZES[c], :].rearrange("p j i s -> p j (i s)"),
                 )
 
-            load_chunk(0)
             nc.sync.dma_start(
                 out=g_raw.rearrange("p b j t e g -> p b (j t e g)"),
                 in_=grad_out.rearrange("b (p j) t g -> p b (j t g)", j=PACK),
             )
-            for c in range(1, CHUNKS):
+            for c in range(CHUNKS):
                 load_chunk(c)
 
             nc.vector.memset(g_grouped[:, :, 0, :, 0, :], 0.0)
@@ -205,34 +204,32 @@ def tile_svconv2d_pa_s_kernel(tc, x, kernel, bias, grad_out, out):
                     if h == HALVES - 1:
                         multiply(g, m)
 
-            vector_share(0)
-            scalar_share(0)
             regroup_grad(0)
             regroup_grad(1)
             nc.vector.tensor_copy(out=g_grouped[:, :, 3, :, 0 : TH - 1, :], in_=g_grouped[:, :, 1, :, 1:TH, :])
             nc.vector.tensor_copy(out=g_grouped[:, :, 0, :, 1:TH, :], in_=g_grouped[:, :, 2, :, 0 : TH - 1, :])
-            scalar_share(1)
+            scalar_share(0)
             nc.vector.quantize_mx(
                 out=g_codes.rearrange("p g k c -> p (g k c)").bitcast(E5M2_X4),
                 scales=g_scales.rearrange("p g k c -> p (g k c)"),
                 in_=g_grouped.rearrange("p g k b t j -> p (g k b t j)"),
             )
+            vector_share(0)
             vector_share(1)
-            vector_share(2)
-            scalar_share(2)
+            scalar_share(1)
             quantise(own, 0)
             quantise(early, 0)
-            keep_clock_up(3, 3)
-            vector_share(3)
-            scalar_share(3)
+            keep_clock_up(2, 3)
+            vector_share(2)
+            scalar_share(2)
             quantise(late, 0)
-            keep_clock_up(4, 2)
+            keep_clock_up(LAST, 2)
             for k in range(2, 7):
-                scalar_runs(4, k, k + 1)
-            vector_pairs(4, 0, 1)
-            vector_singles(4)
+                scalar_runs(LAST, k, k + 1)
+            vector_pairs(LAST, 0, 1)
+            vector_singles(LAST)
             quantise(pairs[0:2], 1)
-            vector_pairs(4, TAPS - 2 * KW, 0)
+            vector_pairs(LAST, TAPS - 2 * KW, 0)
             quantise(pairs[2:], 1)
 
             for f in range(F):

@@ -49,8 +49,8 @@ def tile_svconv2d_pa_s_kernel(tc, x, kernel, bias, grad_out, out):
     with tc.tile_pool(name="keep", bufs=1) as keep, tc.psum_pool(name="psum", bufs=1) as psum:
         g_raw = keep.tile([P, B, PACK, TH, 2, F], BF16)
         g_grouped = keep.tile([P, F, 4, B, TH, PACK], BF16, align_bytes=64)
-        g_codes = keep.tile([P, F, 4, BLOCK], U32, align_bytes=64)
-        g_scales = keep.tile([P, F, 4, BLOCK], U8, align_bytes=64)
+        g_codes = keep.tile([P, F, 4, BLOCK], U32, align_bytes=256)
+        g_scales = keep.tile([P, F, 4, BLOCK], U8, align_bytes=256)
 
         w_raw = [
             keep.tile([P, PACK, CHUNK_SIZES[c] * F * KH * KW], BF16, name="w_raw%d" % c)
@@ -59,8 +59,8 @@ def tile_svconv2d_pa_s_kernel(tc, x, kernel, bias, grad_out, out):
         w_grouped = [
             keep.tile([P, TAPS, HALF, PACK], BF16, name="w_grouped%d" % h, align_bytes=64) for h in range(HALVES)
         ]
-        w_codes = keep.tile([P, F, KH, HALVES, F, HALF], U32, align_bytes=64)
-        w_scales = keep.tile([P, F, KH, HALVES, F, HALF], U8, align_bytes=64)
+        w_codes = keep.tile([P, F, KH, HALVES, F, HALF], U32, align_bytes=256)
+        w_scales = keep.tile([P, F, KH, HALVES, F, HALF], U8, align_bytes=256)
 
         identity = keep.tile([P, P], F32)
         sums = keep.tile([P, F, CIN], F32)

import concourse.mybir as mybir
from concourse.masks import make_identity

BF16 = mybir.dt.bfloat16
F32 = mybir.dt.float32
I32 = mybir.dt.int32
U32 = mybir.dt.uint32
U8 = mybir.dt.uint8
E4M3_X4 = mybir.dt.float8_e4m3fn_x4
E5M2_X4 = mybir.dt.float8_e5m2_x4

P = 128
PACK = 4
B, CIN, COUT, T, F, KH, KW = 2, 128, 512, 64, 4, 3, 3
COLS = B * T
TH = T // 2
BLOCK = B * TH

HALF = 64
HALVES = CIN // HALF
CHUNK_SIZES = (32, 32, 32, 32)
CHUNK_STARTS = tuple(sum(CHUNK_SIZES[:c]) for c in range(len(CHUNK_SIZES)))
CHUNKS = len(CHUNK_SIZES)
LAST = CHUNKS - 1

TAPS = F * KH * KW
RUN = 4
VECTOR_TAKES_RUN_6 = (1, 2)
SCALAR_RUNS = (2, 7)

FLOPS = 2 * 30 * COUT * CIN * COLS
BYTES = 2 * B * COUT * T * F + 2 * 30 * COUT * CIN + 4 * B * CIN * T * F


def first_tap(g):
    return max(0, 1 - g)


def tap_count(g):
    return min(KW, F + 1 - g) - first_tap(g)


def first_out_bin(g):
    return g + first_tap(g) - 1


def tile_svconv2d_pa_s_kernel(tc, x, kernel, bias, grad_out, out):
    nc = tc.nc
    with tc.tile_pool(name="keep", bufs=1) as keep, tc.psum_pool(name="psum", bufs=1) as psum:
        g_raw = keep.tile([P, B, PACK, TH, 2, F], BF16)
        g_grouped = keep.tile([P, F, 4, B, TH, PACK], BF16, align_bytes=64)
        g_codes = keep.tile([P, F, 4, BLOCK], U32, align_bytes=256)
        g_scales = keep.tile([P, F, 4, BLOCK], U8, align_bytes=256)

        w_raw = [
            keep.tile([P, PACK, CHUNK_SIZES[c] * F * KH * KW], BF16, name="w_raw%d" % c)
            for c in range(CHUNKS)
        ]
        w_grouped = [
            keep.tile([P, TAPS, HALF, PACK], BF16, name="w_grouped%d" % h, align_bytes=64) for h in range(HALVES)
        ]
        w_codes = keep.tile([P, F, KH, HALVES, F, HALF], U32, align_bytes=256)
        w_scales = keep.tile([P, F, KH, HALVES, F, HALF], U8, align_bytes=256)

        identity = keep.tile([P, P], F32)
        sums = keep.tile([P, F, CIN], F32)
        result = keep.tile([P, B, TH, 2, F], F32)
        acc = psum.tile([P, HALVES, F, HALF], F32)
        flipped = psum.tile([P, F, 2, B, TH], F32)
        idle_bank = psum.tile([P, 512], F32)

        with tc.manual_schedule():
            kernel_rows = kernel.rearrange("(p j) i g m n -> p j i (g m n)", j=PACK)

            def load_chunk(c):
                i0 = CHUNK_STARTS[c]
                nc.sync.dma_start(
                    out=w_raw[c][:],
                    in_=kernel_rows[:, :, i0 : i0 + CHUNK_SIZES[c], :].rearrange("p j i s -> p j (i s)"),
                )

            nc.sync.dma_start(
                out=g_raw.rearrange("p b j t e g -> p b (j t e g)"),
                in_=grad_out.rearrange("b (p j) t g -> p b (j t g)", j=PACK),
            )
            for c in range(CHUNKS):
                load_chunk(c)

            nc.vector.memset(g_grouped[:, :, 0, :, 0, :], 0.0)
            nc.vector.memset(g_grouped[:, :, 3, :, TH - 1, :], 0.0)
            make_identity(nc, identity[:])
            for g in range(F):
                lo, hi = first_out_bin(g), first_out_bin(g) + tap_count(g)
                for f0, f1 in ((0, lo), (hi, F)):
                    if f0 < f1:
                        empty_codes = w_codes[:, g, :, :, f0:f1, :].rearrange("p m h f i -> p (m h) (f i)")
                        if g in (1, 2):
                            nc.gpsimd.memset(empty_codes.bitcast(F32), 0.0)
                        else:
                            nc.vector.memset(empty_codes.bitcast(I32), 0)
                        nc.vector.memset(
                            w_scales[:, g, :, :, f0:f1, :].rearrange("p m h f i -> p (m h) (f i)").bitcast(I32), 0
                        )

            def views(c):
                h, i0 = divmod(CHUNK_STARTS[c], HALF)
                src = w_raw[c].rearrange("p j (i s) -> p j i s", s=TAPS)
                dst = w_grouped[h][:, :, i0 : i0 + CHUNK_SIZES[c], :]
                return src, dst

            def scalar_runs(c, k0, k1):
                src, dst = views(c)
                nc.scalar.copy(
                    out=dst[:, RUN * k0 : RUN * k1].rearrange("p (k q) i j -> p k i j q", q=RUN),
                    in_=src[:, :, :, RUN * k0 : RUN * k1].rearrange("p j i (k q) -> p k i j q", q=RUN),
                )

            def vector_pairs(c, s0, n0):
                src, dst = views(c)
                nc.vector.tensor_copy(
                    out=dst[:, s0 : s0 + 2 * KW].rearrange("p (m n) i j -> p m i j n", n=KW)[:, :, :, :, n0 : n0 + 2],
                    in_=src[:, :, :, s0 : s0 + 2 * KW].rearrange("p j i (m n) -> p m i j n", n=KW)[:, :, :, :, n0 : n0 + 2],
                )

            def vector_singles(c):
                src, dst = views(c)
                nc.vector.tensor_copy(
                    out=dst[:, 7:TAPS:21],
                    in_=src[:, :, :, 7:TAPS:21].rearrange("p j i x -> p x i j"),
                )

            def quantise_half(g, m, h):
                s0 = (g * KH + m) * KW + first_tap(g)
                for n0 in range(0, tap_count(g), 2):
                    n1 = min(n0 + 2, tap_count(g))
                    f0, f1 = first_out_bin(g) + n0, first_out_bin(g) + n1
                    nc.vector.quantize_mx(
                        out=w_codes[:, g, m, h, f0:f1, :].rearrange("p f i -> p (f i)").bitcast(E4M3_X4),
                        scales=w_scales[:, g, m, h, f0:f1, :].rearrange("p f i -> p (f i)"),
                        in_=w_grouped[h][:, s0 + n0 : s0 + n1].rearrange("p n i j -> p (n i j)"),
                    )

            own = [(0, 0), (0, 1), (3, 1), (3, 2)]
            early = [(0, 2), (1, 0), (1, 1)]
            late = [(1, 2), (2, 0), (2, 1), (2, 2), (3, 0)]
            pairs = own[0:2] + early[0:1] + own[2:4] + early[1:3] + late

            def multiply(g, m):
                nc.tensor.matmul_mx(
                    out=acc[:].rearrange("p h f i -> p (h f i)"),
                    lhsT=g_codes[:, g, 2 - m : 4 - m, :].rearrange("p k c -> p (k c)").bitcast(E5M2_X4),
                    lhsT_scale=g_scales[:, g, 2 - m : 4 - m, :].rearrange("p k c -> p (k c)"),
                    rhs=w_codes[:, g, m].rearrange("p h f i -> p (h f i)").bitcast(E4M3_X4),
                    rhs_scale=w_scales[:, g, m].rearrange("p h f i -> p (h f i)"),
                    start=((g, m) == pairs[0]),
                    stop=((g, m) == pairs[-1]),
                )

            def regroup_grad(e):
                dst = g_grouped[:, :, 1 + e].rearrange("p g b t j -> p b t j g")
                src = g_raw[:, :, :, :, e, :].rearrange("p b j t g -> p b t j g")
                if e == 0:
                    nc.vector.tensor_copy(out=dst, in_=src)
                else:
                    nc.scalar.copy(out=dst, in_=src)

            def quantise_bin(g, h):
                for m in range(KH):
                    quantise_half(g, m, h)
                    if h == HALVES - 1:
                        multiply(g, m)

            def keep_clock_up(c, products):
                for j in range(products):
                    nc.tensor.matmul(
                        out=idle_bank[:, 0:P],
                        lhsT=identity[:],
                        rhs=w_raw[c][:, j, 0 : 2 * P].bitcast(F32),
                        start=True,
                        stop=True,
                    )

            def vector_run(c, k):
                src, dst = views(c)
                nc.vector.tensor_copy(
                    out=dst[:, RUN * k : RUN * (k + 1)].rearrange("p q i j -> p i j q"),
                    in_=src[:, :, :, RUN * k : RUN * (k + 1)].rearrange("p j i q -> p i j q"),
                )

            def vector_share(c):
                vector_pairs(c, 0, 1)
                vector_pairs(c, TAPS - 2 * KW, 0)
                vector_singles(c)
                if c in VECTOR_TAKES_RUN_6:
                    vector_run(c, 6)

            def scalar_share(c):
                scalar_runs(c, 2, 4)
                scalar_runs(c, 4, 6 if c in VECTOR_TAKES_RUN_6 else 7)

            def quantise(units, h):
                for g, m in units:
                    quantise_half(g, m, h)
                    if h == HALVES - 1:
                        multiply(g, m)

            regroup_grad(0)
            regroup_grad(1)
            nc.vector.tensor_copy(out=g_grouped[:, :, 3, :, 0 : TH - 1, :], in_=g_grouped[:, :, 1, :, 1:TH, :])
            nc.vector.tensor_copy(out=g_grouped[:, :, 0, :, 1:TH, :], in_=g_grouped[:, :, 2, :, 0 : TH - 1, :])
            scalar_share(0)
            nc.vector.quantize_mx(
                out=g_codes.rearrange("p g k c -> p (g k c)").bitcast(E5M2_X4),
                scales=g_scales.rearrange("p g k c -> p (g k c)"),
                in_=g_grouped.rearrange("p g k b t j -> p (g k b t j)"),
            )
            vector_share(0)
            vector_share(1)
            scalar_share(1)
            quantise(own, 0)
            quantise(early, 0)
            keep_clock_up(2, 3)
            vector_share(2)
            scalar_share(2)
            quantise(late, 0)
            keep_clock_up(LAST, 2)
            for k in range(2, 7):
                scalar_runs(LAST, k, k + 1)
            vector_pairs(LAST, 0, 1)
            vector_singles(LAST)
            quantise(pairs[0:2], 1)
            vector_pairs(LAST, TAPS - 2 * KW, 0)
            quantise(pairs[2:], 1)

            for f in range(F):
                nc.vector.tensor_copy(
                    out=sums[:, f, :].rearrange("p (h i) -> p h i", h=HALVES), in_=acc[:, :, f, :]
                )
                nc.tensor.transpose(flipped[:, f].rearrange("p e b t -> p (e b t)"), sums[:, f, :], identity[:])
            for b in range(B):
                nc.vector.tensor_copy(
                    out=result[:, b], in_=flipped[:, :, :, b, :].rearrange("p f e t -> p t e f")
                )
                nc.sync.dma_start(
                    out=out[b].rearrange("i t f -> i (t f)"), in_=result[:, b].rearrange("p t e f -> p (t e f)")
                )
